import numpy as np
import ml_dtypes


def mxq(x, axis, fmt="e4m3"):
    dtype, down = {"e4m3": (ml_dtypes.float8_e4m3fn, 7), "e5m2": (ml_dtypes.float8_e5m2, 14)}[fmt]
    v = np.moveaxis(np.asarray(x, np.float32).astype(ml_dtypes.bfloat16).astype(np.float64), axis, -1)
    blocks = v.reshape(v.shape[:-1] + (-1, 32))
    amax = np.abs(blocks).max(-1, keepdims=True)
    byte = np.maximum(np.where(amax > 0, np.frexp(amax)[1] - 1 + 127, 0) - down, 1)
    scale = np.exp2(byte - 127.0)
    codes = (blocks / scale).astype(np.float32).astype(dtype).astype(np.float64)
    return np.moveaxis((codes * scale).reshape(v.shape), -1, axis)


WIDE = False


def mx_kscale(k):
    if not WIDE:
        return np.ones(k)
    levels = np.array([20, -20, 10, -10, 0])
    a = np.random.permutation(np.resize(levels, k // 512 * 4)).reshape(k // 512, 4)
    idx = np.arange(k)
    return np.exp2(a[idx // 512, idx % 128 // 32])


BF16 = ml_dtypes.bfloat16


def bf(x):
    return np.asarray(x, np.float32).astype(BF16)


def f64(x):
    return np.asarray(x).astype(np.float64)


B, IN, L = 512, 1024, 1024


def sigmoid(v):
    return 1.0 / (1.0 + np.exp(-v))


def gates(input, gh0, W_ih0, b_ih0):
    gh = f64(gh0)
    gi = f64(input) @ f64(W_ih0).T + f64(b_ih0)
    r = sigmoid(gi[:, :L] + gh[:, :L])
    z = sigmoid(gi[:, L:2 * L] + gh[:, L:2 * L])
    n = np.tanh(gi[:, 2 * L:] + r * gh[:, 2 * L:])
    return r, z, n


def setup_inputs():
    s = mx_kscale(B)[:, None]
    input0 = bf(np.random.standard_normal((B, IN)))
    h0 = bf(np.random.standard_normal((B, L)))
    gh0 = bf(np.random.standard_normal((B, 3 * L)) * 0.75)
    W_ih0 = bf(np.random.standard_normal((3 * L, IN)) * 0.7 / np.sqrt(IN))
    b_ih0 = bf(np.random.standard_normal(3 * L) * 0.3)
    g = bf(np.random.standard_normal((B, L)) * np.exp2(np.random.randint(-12, 1, (B, 1))) * 4.0 / s)
    r, z, n = gates(input0, gh0, W_ih0, b_ih0)
    return {"input": bf(f64(input0) * s), "h0": h0, "gh0": gh0, "W_ih0": W_ih0, "b_ih0": b_ih0,
            "r": np.asarray(r, np.float32), "z": np.asarray(z, np.float32), "n": np.asarray(n, np.float32),
            "grad_out": g}


def reference(input, h0, gh0, W_ih0, b_ih0, r, z, n, grad_out):
    g, h = f64(grad_out), f64(h0)
    h_n = f64(gh0)[:, 2 * L:]
    rf, zf, nf = f64(r), f64(z), f64(n)
    dn = g * (1.0 - zf) * (1.0 - nf * nf)
    dz = g * (h - nf) * zf * (1.0 - zf)
    dr = dn * h_n * rf * (1.0 - rf)
    dgi = np.concatenate([dr, dz, dn], axis=1)
    return mxq(dgi, 0, "e5m2").T @ mxq(f64(input), 0, "e4m3")

@@ -1,0 +1,159 @@
+from contextlib import ExitStack
+
+import concourse.mybir as mybir
+
+F32 = mybir.dt.float32
+BF16 = mybir.dt.bfloat16
+U32 = mybir.dt.uint32
+U8 = mybir.dt.uint8
+E4M3X4 = mybir.dt.float8_e4m3fn_x4
+E5M2X4 = mybir.dt.float8_e5m2_x4
+ALU = mybir.AluOpType
+ACT = mybir.ActivationFunctionType
+
+P = 128
+PACK = 4
+TOKENS = P * PACK
+L = 1024
+IN = 1024
+CW = 256
+ROUNDS = L // CW
+M_TILE = 128
+N_TILE = 512
+
+FLOPS = 2 * TOKENS * 3 * L * IN
+BYTES = 2 * TOKENS * (IN + 3 * L) + 4 * TOKENS * 3 * L + 4 * 3 * L * IN
+
+
+def by_partition(dram):
+    return dram.rearrange("(p j) w -> p j w", j=PACK)
+
+
+def grouped_view(natural):
+    return natural.rearrange("p j w -> p w j")
+
+
+def tile_grucellstack_pa_v_kernel(tc, x, h0, gh0, w_ih0, b_ih0, r, z, n, grad_out, out):
+    nc = tc.nc
+    with ExitStack() as stack:
+        keep = stack.enter_context(tc.tile_pool(name="keep", bufs=1))
+        work = stack.enter_context(tc.tile_pool(name="work", bufs=2))
+        rows = stack.enter_context(tc.tile_pool(name="rows", bufs=3))
+        banks = stack.enter_context(tc.psum_pool(name="banks", bufs=8))
+
+        z_sb = keep.tile([P, PACK, L], F32)
+        g_sb = keep.tile([P, PACK, L], BF16)
+        x_sb = keep.tile([P, PACK, IN], BF16)
+        n_sb = keep.tile([P, PACK, L], F32)
+        h_sb = keep.tile([P, PACK, L], BF16)
+        r_sb = keep.tile([P, PACK, L], F32)
+        ghn_sb = keep.tile([P, PACK, L], BF16)
+
+        def load(tile, dram, pieces):
+            width = L // pieces
+            for i in range(pieces):
+                cols = slice(i * width, (i + 1) * width)
+                nc.sync.dma_start(out=tile[:, :, cols], in_=by_partition(dram)[:, :, cols])
+
+        half = L // 2
+        for cols in (slice(0, half), slice(half, L)):
+            nc.sync.dma_start(out=z_sb[:, :, cols], in_=by_partition(z)[:, :, cols])
+            nc.sync.dma_start(out=g_sb[:, :, cols], in_=by_partition(grad_out)[:, :, cols])
+        load(x_sb, x, 1)
+        load(n_sb, n, 2)
+        load(h_sb, h0, 1)
+        load(r_sb, r, 1)
+        load(ghn_sb, gh0[:, 2 * L : 3 * L], 1)
+
+        x_grouped = keep.tile([P, IN, PACK], BF16, align_bytes=64)
+        x_codes = keep.tile([P, IN], U32, align_bytes=64)
+        x_scales = keep.tile([P, IN], U8, align_bytes=64)
+        for i in range(IN // N_TILE):
+            cols = slice(i * N_TILE, (i + 1) * N_TILE)
+            nc.scalar.copy(out=x_grouped[:, cols, :], in_=grouped_view(x_sb[:, :, cols]))
+        for i in range(IN // N_TILE):
+            cols = slice(i * N_TILE, (i + 1) * N_TILE)
+            nc.vector.quantize_mx(
+                out=x_codes[:, cols].bitcast(E4M3X4),
+                scales=x_scales[:, cols],
+                in_=x_grouped[:, cols, :].rearrange("p w j -> p (w j)"),
+            )
+
+        dgi_codes = keep.tile([P, 3 * L], U32, align_bytes=64)
+        dgi_scales = keep.tile([P, 3 * L], U8, align_bytes=64)
+
+        def multiply_and_store(first_row, grouped):
+            cols = slice(first_row, first_row + CW)
+            nc.vector.quantize_mx(
+                out=dgi_codes[:, cols].bitcast(E5M2X4),
+                scales=dgi_scales[:, cols],
+                in_=grouped[:].rearrange("p w j -> p (w j)"),
+            )
+            out_rows = rows.tile([P, CW // M_TILE, IN], F32)
+            for t in range(CW // M_TILE):
+                m_cols = slice(first_row + t * M_TILE, first_row + (t + 1) * M_TILE)
+                for i in range(IN // N_TILE):
+                    n_cols = slice(i * N_TILE, (i + 1) * N_TILE)
+                    acc = banks.tile([M_TILE, N_TILE], F32)
+                    nc.tensor.matmul_mx(
+                        out=acc[:],
+                        lhsT=dgi_codes[:, m_cols].bitcast(E5M2X4),
+                        lhsT_scale=dgi_scales[:, m_cols],
+                        rhs=x_codes[:, n_cols].bitcast(E4M3X4),
+                        rhs_scale=x_scales[:, n_cols],
+                        start=True,
+                        stop=True,
+                    )
+                    nc.scalar.copy(out=out_rows[:, t, n_cols], in_=acc[:])
+            nc.sync.dma_start(
+                out=out[cols, :].rearrange("(t p) c -> p t c", p=P), in_=out_rows[:]
+            )
+
+        a_sb = keep.tile([P, PACK, L], F32)
+        az_sb = keep.tile([P, PACK, L], F32)
+        for c in range(ROUNDS):
+            cols = slice(c * CW, (c + 1) * CW)
+            nc.vector.scalar_tensor_tensor(
+                out=a_sb[:, :, cols], in0=z_sb[:, :, cols], scalar=1.0, in1=g_sb[:, :, cols],
+                op0=ALU.subtract, op1=ALU.mult,
+            )
+            nc.vector.tensor_mul(out=az_sb[:, :, cols], in0=a_sb[:, :, cols], in1=z_sb[:, :, cols])
+
+        dn_sb = keep.tile([P, L, PACK], F32)
+        for c in range(ROUNDS):
+            cols = slice(c * CW, (c + 1) * CW)
+            nn = work.tile([P, PACK, CW], F32)
+            nc.scalar.activation(out=nn[:], in_=n_sb[:, :, cols], func=ACT.Square)
+            nc.vector.scalar_tensor_tensor(
+                out=dn_sb[:, cols, :], in0=grouped_view(nn[:]), scalar=1.0,
+                in1=grouped_view(a_sb[:, :, cols]), op0=ALU.subtract, op1=ALU.mult,
+            )
+            grouped = work.tile([P, CW, PACK], BF16, align_bytes=64)
+            nc.scalar.copy(out=grouped[:], in_=dn_sb[:, cols, :])
+            multiply_and_store(2 * L + c * CW, grouped)
+
+        for c in range(ROUNDS):
+            cols = slice(c * CW, (c + 1) * CW)
+            nh = work.tile([P, PACK, CW], F32)
+            nc.vector.tensor_sub(out=nh[:], in0=n_sb[:, :, cols], in1=h_sb[:, :, cols])
+            grouped = work.tile([P, CW, PACK], BF16, align_bytes=64)
+            nc.vector.tensor_mul(
+                out=grouped[:], in0=grouped_view(nh[:]), in1=grouped_view(az_sb[:, :, cols])
+            )
+            multiply_and_store(L + c * CW, grouped)
+
+        for c in range(ROUNDS):
+            cols = slice(c * CW, (c + 1) * CW)
+            rr = work.tile([P, PACK, CW], F32)
+            nc.vector.scalar_tensor_tensor(
+                out=rr[:], in0=r_sb[:, :, cols], scalar=1.0, in1=r_sb[:, :, cols],
+                op0=ALU.subtract, op1=ALU.mult,
+            )
+            rrg = work.tile([P, PACK, CW], F32)
+            nc.vector.tensor_mul(out=rrg[:], in0=rr[:], in1=ghn_sb[:, :, cols])
+            grouped = work.tile([P, CW, PACK], BF16, align_bytes=64)
+            nc.vector.scalar_tensor_tensor(
+                out=grouped[:], in0=grouped_view(rrg[:]), scalar=-1.0, in1=dn_sb[:, cols, :],
+                op0=ALU.mult, op1=ALU.mult,
+            )
+            multiply_and_store(c * CW, grouped)

@@ -1,6 +1,7 @@
 from contextlib import ExitStack
 
 import concourse.mybir as mybir
+from concourse.masks import make_identity
 
 F32 = mybir.dt.float32
 BF16 = mybir.dt.bfloat16
@@ -38,8 +39,9 @@ def tile_grucellstack_pa_v_kernel(tc, x, h0, gh0, w_ih0, b_ih0, r, z, n, grad_ou
     with ExitStack() as stack:
         keep = stack.enter_context(tc.tile_pool(name="keep", bufs=1))
         work = stack.enter_context(tc.tile_pool(name="work", bufs=2))
-        rows = stack.enter_context(tc.tile_pool(name="rows", bufs=3))
-        banks = stack.enter_context(tc.psum_pool(name="banks", bufs=8))
+        rows = stack.enter_context(tc.tile_pool(name="rows", bufs=6))
+        sums = stack.enter_context(tc.psum_pool(name="sums", bufs=5))
+        diffs = stack.enter_context(tc.psum_pool(name="diffs", bufs=3))
 
         z_sb = keep.tile([P, PACK, L], F32)
         g_sb = keep.tile([P, PACK, L], BF16)
@@ -49,30 +51,32 @@ def tile_grucellstack_pa_v_kernel(tc, x, h0, gh0, w_ih0, b_ih0, r, z, n, grad_ou
         r_sb = keep.tile([P, PACK, L], F32)
         ghn_sb = keep.tile([P, PACK, L], BF16)
 
-        def load(tile, dram, pieces):
-            width = L // pieces
-            for i in range(pieces):
-                cols = slice(i * width, (i + 1) * width)
-                nc.sync.dma_start(out=tile[:, :, cols], in_=by_partition(dram)[:, :, cols])
+        def load(tile, dram, cols):
+            nc.sync.dma_start(out=tile[:, :, cols], in_=by_partition(dram)[:, :, cols])
 
-        half = L // 2
-        for cols in (slice(0, half), slice(half, L)):
-            nc.sync.dma_start(out=z_sb[:, :, cols], in_=by_partition(z)[:, :, cols])
-            nc.sync.dma_start(out=g_sb[:, :, cols], in_=by_partition(grad_out)[:, :, cols])
-        load(x_sb, x, 1)
-        load(n_sb, n, 2)
-        load(h_sb, h0, 1)
-        load(r_sb, r, 1)
-        load(ghn_sb, gh0[:, 2 * L : 3 * L], 1)
+        first_half, second_half, whole = slice(0, L // 2), slice(L // 2, L), slice(0, L)
+        load(z_sb, z, first_half)
+        load(g_sb, grad_out, first_half)
+        load(x_sb, x, whole)
+        load(n_sb, n, first_half)
+        load(z_sb, z, second_half)
+        load(g_sb, grad_out, second_half)
+        load(n_sb, n, second_half)
+        load(h_sb, h0, whole)
+        load(r_sb, r, whole)
+        load(ghn_sb, gh0[:, 2 * L : 3 * L], whole)
+
+        ident = keep.tile([P, P], F32)
+        make_identity(nc, ident[:])
+        neg_ident = keep.tile([P, P], BF16)
+        nc.vector.tensor_scalar_mul(out=neg_ident[:], in0=ident[:], scalar1=-1.0)
 
         x_grouped = keep.tile([P, IN, PACK], BF16, align_bytes=64)
         x_codes = keep.tile([P, IN], U32, align_bytes=64)
         x_scales = keep.tile([P, IN], U8, align_bytes=64)
-        for i in range(IN // N_TILE):
-            cols = slice(i * N_TILE, (i + 1) * N_TILE)
-            nc.scalar.copy(out=x_grouped[:, cols, :], in_=grouped_view(x_sb[:, :, cols]))
-        for i in range(IN // N_TILE):
-            cols = slice(i * N_TILE, (i + 1) * N_TILE)
+        nc.scalar.copy(out=x_grouped[:, first_half, :], in_=grouped_view(x_sb[:, :, first_half]))
+        nc.vector.tensor_copy(out=x_grouped[:, second_half, :], in_=grouped_view(x_sb[:, :, second_half]))
+        for cols in (first_half, second_half):
             nc.vector.quantize_mx(
                 out=x_codes[:, cols].bitcast(E4M3X4),
                 scales=x_scales[:, cols],
@@ -82,19 +86,19 @@ def tile_grucellstack_pa_v_kernel(tc, x, h0, gh0, w_ih0, b_ih0, r, z, n, grad_ou
         dgi_codes = keep.tile([P, 3 * L], U32, align_bytes=64)
         dgi_scales = keep.tile([P, 3 * L], U8, align_bytes=64)
 
-        def multiply_and_store(first_row, grouped):
-            cols = slice(first_row, first_row + CW)
+        def multiply_and_store(first_row, grouped, width, vector_helps):
+            cols = slice(first_row, first_row + width)
             nc.vector.quantize_mx(
                 out=dgi_codes[:, cols].bitcast(E5M2X4),
                 scales=dgi_scales[:, cols],
                 in_=grouped[:].rearrange("p w j -> p (w j)"),
             )
-            out_rows = rows.tile([P, CW // M_TILE, IN], F32)
-            for t in range(CW // M_TILE):
+            for t in range(width // M_TILE):
                 m_cols = slice(first_row + t * M_TILE, first_row + (t + 1) * M_TILE)
+                out_rows = rows.tile([P, IN], F32)
                 for i in range(IN // N_TILE):
                     n_cols = slice(i * N_TILE, (i + 1) * N_TILE)
-                    acc = banks.tile([M_TILE, N_TILE], F32)
+                    acc = sums.tile([M_TILE, N_TILE], F32)
                     nc.tensor.matmul_mx(
                         out=acc[:],
                         lhsT=dgi_codes[:, m_cols].bitcast(E5M2X4),
@@ -104,13 +108,15 @@ def tile_grucellstack_pa_v_kernel(tc, x, h0, gh0, w_ih0, b_ih0, r, z, n, grad_ou
                         start=True,
                         stop=True,
                     )
-                    nc.scalar.copy(out=out_rows[:, t, n_cols], in_=acc[:])
-            nc.sync.dma_start(
-                out=out[cols, :].rearrange("(t p) c -> p t c", p=P), in_=out_rows[:]
-            )
+                    if vector_helps and i == 1:
+                        nc.vector.tensor_copy(out=out_rows[:, n_cols], in_=acc[:])
+                    else:
+                        nc.scalar.copy(out=out_rows[:, n_cols], in_=acc[:])
+                nc.sync.dma_start(out=out[m_cols, :], in_=out_rows[:])
 
         a_sb = keep.tile([P, PACK, L], F32)
         az_sb = keep.tile([P, PACK, L], F32)
+        dn_sb = keep.tile([P, L, PACK], F32)
         for c in range(ROUNDS):
             cols = slice(c * CW, (c + 1) * CW)
             nc.vector.scalar_tensor_tensor(
@@ -118,10 +124,6 @@ def tile_grucellstack_pa_v_kernel(tc, x, h0, gh0, w_ih0, b_ih0, r, z, n, grad_ou
                 op0=ALU.subtract, op1=ALU.mult,
             )
             nc.vector.tensor_mul(out=az_sb[:, :, cols], in0=a_sb[:, :, cols], in1=z_sb[:, :, cols])
-
-        dn_sb = keep.tile([P, L, PACK], F32)
-        for c in range(ROUNDS):
-            cols = slice(c * CW, (c + 1) * CW)
             nn = work.tile([P, PACK, CW], F32)
             nc.scalar.activation(out=nn[:], in_=n_sb[:, :, cols], func=ACT.Square)
             nc.vector.scalar_tensor_tensor(
@@ -130,19 +132,20 @@ def tile_grucellstack_pa_v_kernel(tc, x, h0, gh0, w_ih0, b_ih0, r, z, n, grad_ou
             )
             grouped = work.tile([P, CW, PACK], BF16, align_bytes=64)
             nc.scalar.copy(out=grouped[:], in_=dn_sb[:, cols, :])
-            multiply_and_store(2 * L + c * CW, grouped)
+            multiply_and_store(2 * L + c * CW, grouped, CW, False)
 
         for c in range(ROUNDS):
-            cols = slice(c * CW, (c + 1) * CW)
-            nh = work.tile([P, PACK, CW], F32)
-            nc.vector.tensor_sub(out=nh[:], in0=n_sb[:, :, cols], in1=h_sb[:, :, cols])
-            grouped = work.tile([P, CW, PACK], BF16, align_bytes=64)
-            nc.vector.tensor_mul(
-                out=grouped[:], in0=grouped_view(nh[:]), in1=grouped_view(az_sb[:, :, cols])
-            )
-            multiply_and_store(L + c * CW, grouped)
+            for m in range(c * CW // M_TILE, (c + 1) * CW // M_TILE):
+                cols = slice(m * M_TILE, (m + 1) * M_TILE)
+                nh = diffs.tile([P, PACK, M_TILE], F32)
+                nc.tensor.matmul(out=nh[:], lhsT=ident[:], rhs=n_sb[:, :, cols], start=True, stop=False)
+                nc.tensor.matmul(out=nh[:], lhsT=neg_ident[:], rhs=h_sb[:, :, cols], start=False, stop=True)
+                grouped_m = work.tile([P, M_TILE, PACK], BF16, align_bytes=64)
+                nc.vector.tensor_mul(
+                    out=grouped_m[:], in0=grouped_view(nh[:]), in1=grouped_view(az_sb[:, :, cols])
+                )
+                multiply_and_store(L + m * M_TILE, grouped_m, M_TILE, False)
 
-        for c in range(ROUNDS):
             cols = slice(c * CW, (c + 1) * CW)
             rr = work.tile([P, PACK, CW], F32)
             nc.vector.scalar_tensor_tensor(
@@ -156,4 +159,4 @@ def tile_grucellstack_pa_v_kernel(tc, x, h0, gh0, w_ih0, b_ih0, r, z, n, grad_ou
                 out=grouped[:], in0=grouped_view(rrg[:]), scalar=-1.0, in1=dn_sb[:, cols, :],
                 op0=ALU.mult, op1=ALU.mult,
             )
-            multiply_and_store(c * CW, grouped)
+            multiply_and_store(c * CW, grouped, CW, False)

@@ -21,6 +21,8 @@ CW = 256
 ROUNDS = L // CW
 M_TILE = 128
 N_TILE = 512
+M_TILES = L // M_TILE
+AHEAD = 3
 
 FLOPS = 2 * TOKENS * 3 * L * IN
 BYTES = 2 * TOKENS * (IN + 3 * L) + 4 * TOKENS * 3 * L + 4 * 3 * L * IN
@@ -37,11 +39,12 @@ def grouped_view(natural):
 def tile_grucellstack_pa_v_kernel(tc, x, h0, gh0, w_ih0, b_ih0, r, z, n, grad_out, out):
     nc = tc.nc
     with ExitStack() as stack:
+        stack.enter_context(tc.manual_schedule())
         keep = stack.enter_context(tc.tile_pool(name="keep", bufs=1))
         work = stack.enter_context(tc.tile_pool(name="work", bufs=2))
         rows = stack.enter_context(tc.tile_pool(name="rows", bufs=6))
-        sums = stack.enter_context(tc.psum_pool(name="sums", bufs=5))
-        diffs = stack.enter_context(tc.psum_pool(name="diffs", bufs=3))
+        sums = stack.enter_context(tc.psum_pool(name="sums", bufs=8 - AHEAD))
+        diffs = stack.enter_context(tc.psum_pool(name="diffs", bufs=AHEAD))
 
         z_sb = keep.tile([P, PACK, L], F32)
         g_sb = keep.tile([P, PACK, L], BF16)
@@ -74,89 +77,135 @@ def tile_grucellstack_pa_v_kernel(tc, x, h0, gh0, w_ih0, b_ih0, r, z, n, grad_ou
         x_grouped = keep.tile([P, IN, PACK], BF16, align_bytes=64)
         x_codes = keep.tile([P, IN], U32, align_bytes=64)
         x_scales = keep.tile([P, IN], U8, align_bytes=64)
-        nc.scalar.copy(out=x_grouped[:, first_half, :], in_=grouped_view(x_sb[:, :, first_half]))
-        nc.vector.tensor_copy(out=x_grouped[:, second_half, :], in_=grouped_view(x_sb[:, :, second_half]))
-        for cols in (first_half, second_half):
+        dgi_codes = keep.tile([P, 3 * L], U32, align_bytes=64)
+        dgi_scales = keep.tile([P, 3 * L], U8, align_bytes=64)
+        a_sb = keep.tile([P, PACK, L], F32)
+        az_sb = keep.tile([P, PACK, L], F32)
+        dn_sb = keep.tile([P, L, PACK], F32)
+
+        def quantise_x(cols):
             nc.vector.quantize_mx(
                 out=x_codes[:, cols].bitcast(E4M3X4),
                 scales=x_scales[:, cols],
                 in_=x_grouped[:, cols, :].rearrange("p w j -> p (w j)"),
             )
 
-        dgi_codes = keep.tile([P, 3 * L], U32, align_bytes=64)
-        dgi_scales = keep.tile([P, 3 * L], U8, align_bytes=64)
-
-        def multiply_and_store(first_row, grouped, width, vector_helps):
+        def quantise_dgi(first_row, grouped, width):
             cols = slice(first_row, first_row + width)
             nc.vector.quantize_mx(
                 out=dgi_codes[:, cols].bitcast(E5M2X4),
                 scales=dgi_scales[:, cols],
                 in_=grouped[:].rearrange("p w j -> p (w j)"),
             )
-            for t in range(width // M_TILE):
-                m_cols = slice(first_row + t * M_TILE, first_row + (t + 1) * M_TILE)
-                out_rows = rows.tile([P, IN], F32)
-                for i in range(IN // N_TILE):
-                    n_cols = slice(i * N_TILE, (i + 1) * N_TILE)
-                    acc = sums.tile([M_TILE, N_TILE], F32)
-                    nc.tensor.matmul_mx(
-                        out=acc[:],
-                        lhsT=dgi_codes[:, m_cols].bitcast(E5M2X4),
-                        lhsT_scale=dgi_scales[:, m_cols],
-                        rhs=x_codes[:, n_cols].bitcast(E4M3X4),
-                        rhs_scale=x_scales[:, n_cols],
-                        start=True,
-                        stop=True,
-                    )
-                    if vector_helps and i == 1:
-                        nc.vector.tensor_copy(out=out_rows[:, n_cols], in_=acc[:])
-                    else:
-                        nc.scalar.copy(out=out_rows[:, n_cols], in_=acc[:])
-                nc.sync.dma_start(out=out[m_cols, :], in_=out_rows[:])
 
-        a_sb = keep.tile([P, PACK, L], F32)
-        az_sb = keep.tile([P, PACK, L], F32)
-        dn_sb = keep.tile([P, L, PACK], F32)
+        def multiply_and_store(first_row, vector_helps):
+            m_cols = slice(first_row, first_row + M_TILE)
+            out_rows = rows.tile([P, IN], F32)
+            for i in range(IN // N_TILE):
+                n_cols = slice(i * N_TILE, (i + 1) * N_TILE)
+                acc = sums.tile([M_TILE, N_TILE], F32)
+                nc.tensor.matmul_mx(
+                    out=acc[:],
+                    lhsT=dgi_codes[:, m_cols].bitcast(E5M2X4),
+                    lhsT_scale=dgi_scales[:, m_cols],
+                    rhs=x_codes[:, n_cols].bitcast(E4M3X4),
+                    rhs_scale=x_scales[:, n_cols],
+                    start=True,
+                    stop=True,
+                )
+                if vector_helps and i == 1:
+                    nc.vector.tensor_copy(out=out_rows[:, n_cols], in_=acc[:])
+                else:
+                    nc.scalar.copy(out=out_rows[:, n_cols], in_=acc[:])
+            nc.sync.dma_start(out=out[m_cols, :], in_=out_rows[:])
+
+        nh = {}
+
+        def form_difference(m):
+            cols = slice(m * M_TILE, (m + 1) * M_TILE)
+            nh[m] = diffs.tile([P, PACK, M_TILE], F32, name="nh")
+            nc.tensor.matmul(out=nh[m][:], lhsT=ident[:], rhs=n_sb[:, :, cols], start=True, stop=False)
+            nc.tensor.matmul(out=nh[m][:], lhsT=neg_ident[:], rhs=h_sb[:, :, cols], start=False, stop=True)
+
+        nn_sb = keep.tile([P, PACK, L], F32)
+        nc.scalar.copy(out=x_grouped[:, first_half, :], in_=grouped_view(x_sb[:, :, first_half]))
         for c in range(ROUNDS):
             cols = slice(c * CW, (c + 1) * CW)
-            nc.vector.scalar_tensor_tensor(
-                out=a_sb[:, :, cols], in0=z_sb[:, :, cols], scalar=1.0, in1=g_sb[:, :, cols],
-                op0=ALU.subtract, op1=ALU.mult,
-            )
-            nc.vector.tensor_mul(out=az_sb[:, :, cols], in0=a_sb[:, :, cols], in1=z_sb[:, :, cols])
-            nn = work.tile([P, PACK, CW], F32)
-            nc.scalar.activation(out=nn[:], in_=n_sb[:, :, cols], func=ACT.Square)
-            nc.vector.scalar_tensor_tensor(
-                out=dn_sb[:, cols, :], in0=grouped_view(nn[:]), scalar=1.0,
-                in1=grouped_view(a_sb[:, :, cols]), op0=ALU.subtract, op1=ALU.mult,
-            )
-            grouped = work.tile([P, CW, PACK], BF16, align_bytes=64)
-            nc.scalar.copy(out=grouped[:], in_=dn_sb[:, cols, :])
-            multiply_and_store(2 * L + c * CW, grouped, CW, False)
+            nc.scalar.activation(out=nn_sb[:, :, cols], in_=n_sb[:, :, cols], func=ACT.Square)
+
+        for pair in range(ROUNDS // 2):
+            both = (2 * pair, 2 * pair + 1)
+            grouped = {}
+            for c in both:
+                cols = slice(c * CW, (c + 1) * CW)
+                nc.vector.scalar_tensor_tensor(
+                    out=a_sb[:, :, cols], in0=z_sb[:, :, cols], scalar=1.0, in1=g_sb[:, :, cols],
+                    op0=ALU.subtract, op1=ALU.mult,
+                )
+            for c in both:
+                cols = slice(c * CW, (c + 1) * CW)
+                nc.vector.tensor_mul(out=az_sb[:, :, cols], in0=a_sb[:, :, cols], in1=z_sb[:, :, cols])
+            if pair == 0:
+                nc.vector.tensor_copy(
+                    out=x_grouped[:, second_half, :], in_=grouped_view(x_sb[:, :, second_half])
+                )
+                quantise_x(first_half)
+            for c in both:
+                cols = slice(c * CW, (c + 1) * CW)
+                nc.vector.scalar_tensor_tensor(
+                    out=dn_sb[:, cols, :], in0=grouped_view(nn_sb[:, :, cols]), scalar=1.0,
+                    in1=grouped_view(a_sb[:, :, cols]), op0=ALU.subtract, op1=ALU.mult,
+                )
+            if pair == 0:
+                quantise_x(second_half)
+            for c in both:
+                cols = slice(c * CW, (c + 1) * CW)
+                grouped[c] = work.tile([P, CW, PACK], BF16, align_bytes=64, name="grouped")
+                nc.vector.tensor_copy(out=grouped[c][:], in_=dn_sb[:, cols, :])
+            for c in both:
+                quantise_dgi(2 * L + c * CW, grouped[c], CW)
+            for c in both:
+                for t in range(CW // M_TILE):
+                    multiply_and_store(2 * L + c * CW + t * M_TILE, False)
+            if pair == 0:
+                for m in range(AHEAD):
+                    form_difference(m)
 
         for c in range(ROUNDS):
-            for m in range(c * CW // M_TILE, (c + 1) * CW // M_TILE):
-                cols = slice(m * M_TILE, (m + 1) * M_TILE)
-                nh = diffs.tile([P, PACK, M_TILE], F32)
-                nc.tensor.matmul(out=nh[:], lhsT=ident[:], rhs=n_sb[:, :, cols], start=True, stop=False)
-                nc.tensor.matmul(out=nh[:], lhsT=neg_ident[:], rhs=h_sb[:, :, cols], start=False, stop=True)
-                grouped_m = work.tile([P, M_TILE, PACK], BF16, align_bytes=64)
-                nc.vector.tensor_mul(
-                    out=grouped_m[:], in0=grouped_view(nh[:]), in1=grouped_view(az_sb[:, :, cols])
-                )
-                multiply_and_store(L + m * M_TILE, grouped_m, M_TILE, False)
-
+            last_round = c == ROUNDS - 1
             cols = slice(c * CW, (c + 1) * CW)
             rr = work.tile([P, PACK, CW], F32)
+            rrg = work.tile([P, PACK, CW], F32)
+            dr_grouped = work.tile([P, CW, PACK], BF16, align_bytes=64, name="grouped")
+            dz_grouped = {}
+
+            def dz_tile(m):
+                m_cols = slice(m * M_TILE, (m + 1) * M_TILE)
+                dz_grouped[m] = work.tile([P, M_TILE, PACK], BF16, align_bytes=64, name="dz_grouped")
+                nc.vector.tensor_mul(
+                    out=dz_grouped[m][:], in0=grouped_view(nh[m][:]), in1=grouped_view(az_sb[:, :, m_cols])
+                )
+
             nc.vector.scalar_tensor_tensor(
                 out=rr[:], in0=r_sb[:, :, cols], scalar=1.0, in1=r_sb[:, :, cols],
                 op0=ALU.subtract, op1=ALU.mult,
             )
-            rrg = work.tile([P, PACK, CW], F32)
+            dz_tile(2 * c)
             nc.vector.tensor_mul(out=rrg[:], in0=rr[:], in1=ghn_sb[:, :, cols])
-            grouped = work.tile([P, CW, PACK], BF16, align_bytes=64)
+            quantise_dgi(L + 2 * c * M_TILE, dz_grouped[2 * c], M_TILE)
             nc.vector.scalar_tensor_tensor(
-                out=grouped[:], in0=grouped_view(rrg[:]), scalar=-1.0, in1=dn_sb[:, cols, :],
+                out=dr_grouped[:], in0=grouped_view(rrg[:]), scalar=-1.0, in1=dn_sb[:, cols, :],
                 op0=ALU.mult, op1=ALU.mult,
             )
-            multiply_and_store(c * CW, grouped, CW, False)
+            dz_tile(2 * c + 1)
+            quantise_dgi(c * CW, dr_grouped, CW)
+            quantise_dgi(L + (2 * c + 1) * M_TILE, dz_grouped[2 * c + 1], M_TILE)
+
+            multiply_and_store(L + 2 * c * M_TILE, last_round)
+            if 2 * c + AHEAD < M_TILES:
+                form_difference(2 * c + AHEAD)
+            multiply_and_store(c * CW, last_round)
+            multiply_and_store(c * CW + M_TILE, last_round)
+            multiply_and_store(L + (2 * c + 1) * M_TILE, last_round)
+            if 2 * c + 1 + AHEAD < M_TILES:
+                form_difference(2 * c + 1 + AHEAD)

@@ -54,20 +54,17 @@ def tile_grucellstack_pa_v_kernel(tc, x, h0, gh0, w_ih0, b_ih0, r, z, n, grad_ou
         r_sb = keep.tile([P, PACK, L], F32)
         ghn_sb = keep.tile([P, PACK, L], BF16)
 
-        def load(tile, dram, cols):
-            nc.sync.dma_start(out=tile[:, :, cols], in_=by_partition(dram)[:, :, cols])
-
-        first_half, second_half, whole = slice(0, L // 2), slice(L // 2, L), slice(0, L)
-        load(z_sb, z, first_half)
-        load(g_sb, grad_out, first_half)
-        load(x_sb, x, whole)
-        load(n_sb, n, first_half)
-        load(z_sb, z, second_half)
-        load(g_sb, grad_out, second_half)
-        load(n_sb, n, second_half)
-        load(h_sb, h0, whole)
-        load(r_sb, r, whole)
-        load(ghn_sb, gh0[:, 2 * L : 3 * L], whole)
+        first_tokens, last_tokens = slice(0, PACK // 2), slice(PACK // 2, PACK)
+        nc.sync.dma_start(out=z_sb[:, first_tokens, :], in_=by_partition(z)[:, first_tokens, :])
+        nc.sync.dma_start(out=g_sb[:, first_tokens, :], in_=by_partition(grad_out)[:, first_tokens, :])
+        nc.sync.dma_start(out=x_sb[:], in_=by_partition(x))
+        nc.sync.dma_start(out=z_sb[:, last_tokens, :], in_=by_partition(z)[:, last_tokens, :])
+        nc.sync.dma_start(out=g_sb[:, last_tokens, :], in_=by_partition(grad_out)[:, last_tokens, :])
+        nc.sync.dma_start(out=n_sb[:], in_=by_partition(n))
+        nc.sync.dma_start(out=h_sb[:], in_=by_partition(h0))
+        nc.sync.dma_start(out=r_sb[:], in_=by_partition(r))
+        nc.sync.dma_start(out=ghn_sb[:], in_=by_partition(gh0[:, 2 * L : 3 * L]))
+        first_half, second_half = slice(0, IN // 2), slice(IN // 2, IN)
 
         ident = keep.tile([P, P], F32)
         make_identity(nc, ident[:])
@@ -133,31 +130,32 @@ def tile_grucellstack_pa_v_kernel(tc, x, h0, gh0, w_ih0, b_ih0, r, z, n, grad_ou
             cols = slice(c * CW, (c + 1) * CW)
             nc.scalar.activation(out=nn_sb[:, :, cols], in_=n_sb[:, :, cols], func=ACT.Square)
 
+        for tokens in ((0, 1), (2, 3)):
+            for j in tokens:
+                nc.vector.scalar_tensor_tensor(
+                    out=a_sb[:, j, :], in0=z_sb[:, j, :], scalar=1.0, in1=g_sb[:, j, :],
+                    op0=ALU.subtract, op1=ALU.mult,
+                )
+            for j in tokens:
+                nc.vector.tensor_mul(out=az_sb[:, j, :], in0=a_sb[:, j, :], in1=z_sb[:, j, :])
+            if tokens == (0, 1):
+                nc.vector.tensor_copy(
+                    out=x_grouped[:, second_half, :], in_=grouped_view(x_sb[:, :, second_half])
+                )
+                quantise_x(first_half)
+        quantise_x(second_half)
+
+        for m in range(2):
+            form_difference(m)
         for pair in range(ROUNDS // 2):
             both = (2 * pair, 2 * pair + 1)
             grouped = {}
             for c in both:
                 cols = slice(c * CW, (c + 1) * CW)
                 nc.vector.scalar_tensor_tensor(
-                    out=a_sb[:, :, cols], in0=z_sb[:, :, cols], scalar=1.0, in1=g_sb[:, :, cols],
-                    op0=ALU.subtract, op1=ALU.mult,
-                )
-            for c in both:
-                cols = slice(c * CW, (c + 1) * CW)
-                nc.vector.tensor_mul(out=az_sb[:, :, cols], in0=a_sb[:, :, cols], in1=z_sb[:, :, cols])
-            if pair == 0:
-                nc.vector.tensor_copy(
-                    out=x_grouped[:, second_half, :], in_=grouped_view(x_sb[:, :, second_half])
-                )
-                quantise_x(first_half)
-            for c in both:
-                cols = slice(c * CW, (c + 1) * CW)
-                nc.vector.scalar_tensor_tensor(
                     out=dn_sb[:, cols, :], in0=grouped_view(nn_sb[:, :, cols]), scalar=1.0,
                     in1=grouped_view(a_sb[:, :, cols]), op0=ALU.subtract, op1=ALU.mult,
                 )
-            if pair == 0:
-                quantise_x(second_half)
             for c in both:
                 cols = slice(c * CW, (c + 1) * CW)
                 grouped[c] = work.tile([P, CW, PACK], BF16, align_bytes=64, name="grouped")
@@ -168,7 +166,7 @@ def tile_grucellstack_pa_v_kernel(tc, x, h0, gh0, w_ih0, b_ih0, r, z, n, grad_ou
                 for t in range(CW // M_TILE):
                     multiply_and_store(2 * L + c * CW + t * M_TILE, False)
             if pair == 0:
-                for m in range(AHEAD):
+                for m in range(2, AHEAD):
                     form_difference(m)
 
         for c in range(ROUNDS):

from contextlib import ExitStack

import concourse.mybir as mybir
from concourse.masks import make_identity

F32 = mybir.dt.float32
BF16 = mybir.dt.bfloat16
U32 = mybir.dt.uint32
U8 = mybir.dt.uint8
E4M3X4 = mybir.dt.float8_e4m3fn_x4
E5M2X4 = mybir.dt.float8_e5m2_x4
ALU = mybir.AluOpType
ACT = mybir.ActivationFunctionType

P = 128
PACK = 4
TOKENS = P * PACK
L = 1024
IN = 1024
CW = 256
ROUNDS = L // CW
M_TILE = 128
N_TILE = 512
M_TILES = L // M_TILE
AHEAD = 3

FLOPS = 2 * TOKENS * 3 * L * IN
BYTES = 2 * TOKENS * (IN + 3 * L) + 4 * TOKENS * 3 * L + 4 * 3 * L * IN


def by_partition(dram):
    return dram.rearrange("(p j) w -> p j w", j=PACK)


def grouped_view(natural):
    return natural.rearrange("p j w -> p w j")


def tile_grucellstack_pa_v_kernel(tc, x, h0, gh0, w_ih0, b_ih0, r, z, n, grad_out, out):
    nc = tc.nc
    with ExitStack() as stack:
        stack.enter_context(tc.manual_schedule())
        keep = stack.enter_context(tc.tile_pool(name="keep", bufs=1))
        work = stack.enter_context(tc.tile_pool(name="work", bufs=2))
        rows = stack.enter_context(tc.tile_pool(name="rows", bufs=6))
        sums = stack.enter_context(tc.psum_pool(name="sums", bufs=8 - AHEAD))
        diffs = stack.enter_context(tc.psum_pool(name="diffs", bufs=AHEAD))

        z_sb = keep.tile([P, PACK, L], F32)
        g_sb = keep.tile([P, PACK, L], BF16)
        x_sb = keep.tile([P, PACK, IN], BF16)
        n_sb = keep.tile([P, PACK, L], F32)
        h_sb = keep.tile([P, PACK, L], BF16)
        r_sb = keep.tile([P, PACK, L], F32)
        ghn_sb = keep.tile([P, PACK, L], BF16)

        first_tokens, last_tokens = slice(0, PACK // 2), slice(PACK // 2, PACK)
        nc.sync.dma_start(out=z_sb[:, first_tokens, :], in_=by_partition(z)[:, first_tokens, :])
        nc.sync.dma_start(out=g_sb[:, first_tokens, :], in_=by_partition(grad_out)[:, first_tokens, :])
        nc.sync.dma_start(out=x_sb[:], in_=by_partition(x))
        nc.sync.dma_start(out=z_sb[:, last_tokens, :], in_=by_partition(z)[:, last_tokens, :])
        nc.sync.dma_start(out=g_sb[:, last_tokens, :], in_=by_partition(grad_out)[:, last_tokens, :])
        nc.sync.dma_start(out=n_sb[:], in_=by_partition(n))
        nc.sync.dma_start(out=h_sb[:], in_=by_partition(h0))
        nc.sync.dma_start(out=r_sb[:], in_=by_partition(r))
        nc.sync.dma_start(out=ghn_sb[:], in_=by_partition(gh0[:, 2 * L : 3 * L]))
        first_half, second_half = slice(0, IN // 2), slice(IN // 2, IN)

        ident = keep.tile([P, P], F32)
        make_identity(nc, ident[:])
        neg_ident = keep.tile([P, P], BF16)
        nc.vector.tensor_scalar_mul(out=neg_ident[:], in0=ident[:], scalar1=-1.0)

        x_grouped = keep.tile([P, IN, PACK], BF16, align_bytes=64)
        x_codes = keep.tile([P, IN], U32, align_bytes=64)
        x_scales = keep.tile([P, IN], U8, align_bytes=64)
        dgi_codes = keep.tile([P, 3 * L], U32, align_bytes=64)
        dgi_scales = keep.tile([P, 3 * L], U8, align_bytes=64)
        a_sb = keep.tile([P, PACK, L], F32)
        az_sb = keep.tile([P, PACK, L], F32)
        dn_sb = keep.tile([P, L, PACK], F32)

        def quantise_x(cols):
            nc.vector.quantize_mx(
                out=x_codes[:, cols].bitcast(E4M3X4),
                scales=x_scales[:, cols],
                in_=x_grouped[:, cols, :].rearrange("p w j -> p (w j)"),
            )

        def quantise_dgi(first_row, grouped, width):
            cols = slice(first_row, first_row + width)
            nc.vector.quantize_mx(
                out=dgi_codes[:, cols].bitcast(E5M2X4),
                scales=dgi_scales[:, cols],
                in_=grouped[:].rearrange("p w j -> p (w j)"),
            )

        def multiply_and_store(first_row, vector_helps):
            m_cols = slice(first_row, first_row + M_TILE)
            out_rows = rows.tile([P, IN], F32)
            for i in range(IN // N_TILE):
                n_cols = slice(i * N_TILE, (i + 1) * N_TILE)
                acc = sums.tile([M_TILE, N_TILE], F32)
                nc.tensor.matmul_mx(
                    out=acc[:],
                    lhsT=dgi_codes[:, m_cols].bitcast(E5M2X4),
                    lhsT_scale=dgi_scales[:, m_cols],
                    rhs=x_codes[:, n_cols].bitcast(E4M3X4),
                    rhs_scale=x_scales[:, n_cols],
                    start=True,
                    stop=True,
                )
                if vector_helps and i == 1:
                    nc.vector.tensor_copy(out=out_rows[:, n_cols], in_=acc[:])
                else:
                    nc.scalar.copy(out=out_rows[:, n_cols], in_=acc[:])
            nc.sync.dma_start(out=out[m_cols, :], in_=out_rows[:])

        nh = {}

        def form_difference(m):
            cols = slice(m * M_TILE, (m + 1) * M_TILE)
            nh[m] = diffs.tile([P, PACK, M_TILE], F32, name="nh")
            nc.tensor.matmul(out=nh[m][:], lhsT=ident[:], rhs=n_sb[:, :, cols], start=True, stop=False)
            nc.tensor.matmul(out=nh[m][:], lhsT=neg_ident[:], rhs=h_sb[:, :, cols], start=False, stop=True)

        nn_sb = keep.tile([P, PACK, L], F32)
        nc.scalar.copy(out=x_grouped[:, first_half, :], in_=grouped_view(x_sb[:, :, first_half]))
        for c in range(ROUNDS):
            cols = slice(c * CW, (c + 1) * CW)
            nc.scalar.activation(out=nn_sb[:, :, cols], in_=n_sb[:, :, cols], func=ACT.Square)

        for tokens in ((0, 1), (2, 3)):
            for j in tokens:
                nc.vector.scalar_tensor_tensor(
                    out=a_sb[:, j, :], in0=z_sb[:, j, :], scalar=1.0, in1=g_sb[:, j, :],
                    op0=ALU.subtract, op1=ALU.mult,
                )
            for j in tokens:
                nc.vector.tensor_mul(out=az_sb[:, j, :], in0=a_sb[:, j, :], in1=z_sb[:, j, :])
            if tokens == (0, 1):
                nc.vector.tensor_copy(
                    out=x_grouped[:, second_half, :], in_=grouped_view(x_sb[:, :, second_half])
                )
                quantise_x(first_half)
        quantise_x(second_half)

        for m in range(2):
            form_difference(m)
        for pair in range(ROUNDS // 2):
            both = (2 * pair, 2 * pair + 1)
            grouped = {}
            for c in both:
                cols = slice(c * CW, (c + 1) * CW)
                nc.vector.scalar_tensor_tensor(
                    out=dn_sb[:, cols, :], in0=grouped_view(nn_sb[:, :, cols]), scalar=1.0,
                    in1=grouped_view(a_sb[:, :, cols]), op0=ALU.subtract, op1=ALU.mult,
                )
            for c in both:
                cols = slice(c * CW, (c + 1) * CW)
                grouped[c] = work.tile([P, CW, PACK], BF16, align_bytes=64, name="grouped")
                nc.vector.tensor_copy(out=grouped[c][:], in_=dn_sb[:, cols, :])
            for c in both:
                quantise_dgi(2 * L + c * CW, grouped[c], CW)
            for c in both:
                for t in range(CW // M_TILE):
                    multiply_and_store(2 * L + c * CW + t * M_TILE, False)
            if pair == 0:
                for m in range(2, AHEAD):
                    form_difference(m)

        for c in range(ROUNDS):
            last_round = c == ROUNDS - 1
            cols = slice(c * CW, (c + 1) * CW)
            rr = work.tile([P, PACK, CW], F32)
            rrg = work.tile([P, PACK, CW], F32)
            dr_grouped = work.tile([P, CW, PACK], BF16, align_bytes=64, name="grouped")
            dz_grouped = {}

            def dz_tile(m):
                m_cols = slice(m * M_TILE, (m + 1) * M_TILE)
                dz_grouped[m] = work.tile([P, M_TILE, PACK], BF16, align_bytes=64, name="dz_grouped")
                nc.vector.tensor_mul(
                    out=dz_grouped[m][:], in0=grouped_view(nh[m][:]), in1=grouped_view(az_sb[:, :, m_cols])
                )

            nc.vector.scalar_tensor_tensor(
                out=rr[:], in0=r_sb[:, :, cols], scalar=1.0, in1=r_sb[:, :, cols],
                op0=ALU.subtract, op1=ALU.mult,
            )
            dz_tile(2 * c)
            nc.vector.tensor_mul(out=rrg[:], in0=rr[:], in1=ghn_sb[:, :, cols])
            quantise_dgi(L + 2 * c * M_TILE, dz_grouped[2 * c], M_TILE)
            nc.vector.scalar_tensor_tensor(
                out=dr_grouped[:], in0=grouped_view(rrg[:]), scalar=-1.0, in1=dn_sb[:, cols, :],
                op0=ALU.mult, op1=ALU.mult,
            )
            dz_tile(2 * c + 1)
            quantise_dgi(c * CW, dr_grouped, CW)
            quantise_dgi(L + (2 * c + 1) * M_TILE, dz_grouped[2 * c + 1], M_TILE)

            multiply_and_store(L + 2 * c * M_TILE, last_round)
            if 2 * c + AHEAD < M_TILES:
                form_difference(2 * c + AHEAD)
            multiply_and_store(c * CW, last_round)
            multiply_and_store(c * CW + M_TILE, last_round)
            multiply_and_store(L + (2 * c + 1) * M_TILE, last_round)
            if 2 * c + 1 + AHEAD < M_TILES:
                form_difference(2 * c + 1 + AHEAD)
